import numpy as np
import ml_dtypes


def mxq(x, axis, fmt="e4m3"):
    dtype, down = {"e4m3": (ml_dtypes.float8_e4m3fn, 7), "e5m2": (ml_dtypes.float8_e5m2, 14)}[fmt]
    v = np.moveaxis(np.asarray(x, np.float32).astype(ml_dtypes.bfloat16).astype(np.float64), axis, -1)
    blocks = v.reshape(v.shape[:-1] + (-1, 32))
    amax = np.abs(blocks).max(-1, keepdims=True)
    byte = np.maximum(np.where(amax > 0, np.frexp(amax)[1] - 1 + 127, 0) - down, 1)
    scale = np.exp2(byte - 127.0)
    codes = (blocks / scale).astype(np.float32).astype(dtype).astype(np.float64)
    return np.moveaxis((codes * scale).reshape(v.shape), -1, axis)


WIDE = False


def mx_kscale(k):
    if not WIDE:
        return np.ones(k)
    levels = np.array([10, -10, 5, -5, 0])
    a = np.random.permutation(np.resize(levels, k // 512 * 4)).reshape(k // 512, 4)
    idx = np.arange(k)
    return np.exp2(a[idx // 512, idx % 128 // 32])


BF16 = ml_dtypes.bfloat16


def bf(x):
    return np.asarray(x, np.float32).astype(BF16)


def f64(x):
    return np.asarray(x).astype(np.float64)


B, A, C, P = 64, 7, 1024, 1024
N = A * A + 1


def scramble(y):
    return y.transpose(0, 2, 1).reshape(B, N, C)


def unscramble(z):
    return z.reshape(B, C, N).transpose(0, 2, 1)


def setup_inputs():
    s = mx_kscale(C)
    z = np.random.standard_normal((B, N, C)) * 1.6 / np.sqrt(N) * s
    return {"y_attn": bf(np.ascontiguousarray(unscramble(z))),
            "w_proj": bf(np.random.standard_normal((P, C)) * 2.0 / np.sqrt(C) / s),
            "b_proj": bf(np.random.standard_normal(P) * 0.1)}


def reference(y_attn, w_proj, b_proj):
    z = scramble(f64(y_attn))
    return (mxq(z, 2, "e4m3") @ mxq(f64(w_proj), 1, "e4m3").T) + f64(b_proj)

@@ -1,0 +1,172 @@
+import concourse.mybir as mybir
+from concourse.masks import make_identity
+
+F32 = mybir.dt.float32
+BF16 = mybir.dt.bfloat16
+U32 = mybir.dt.uint32
+U8 = mybir.dt.uint8
+FP8X4 = mybir.dt.float8_e4m3fn_x4
+ADD = mybir.AluOpType.add
+MULT = mybir.AluOpType.mult
+
+P = 128
+IMAGES = 64
+TOKENS = 50
+CHANNELS = 1024
+FEATURES = 1024
+K = 1024
+HALVES = 2
+HALF_CHANNELS = CHANNELS // HALVES
+ROWS = TOKENS // HALVES
+PACK = 4
+K_PASS = P * PACK
+PASSES = K // K_PASS
+WORDS = K // 2
+PLANES = WORDS // P
+N_TILE = 512
+N_TILES = FEATURES // N_TILE
+W_TILES = FEATURES // P
+CHUNKS = (128, 128, 256)
+UNIT = 32
+RUN = 4
+GROUP = 2
+LEAD = 2
+
+FLOPS = 2 * IMAGES * TOKENS * K * FEATURES
+
+
+def transpose_row_tile(nc, bank, rows_bf16, identity):
+    words = rows_bf16.bitcast(F32)
+    for v in range(PLANES):
+        nc.tensor.transpose(bank[:, v, :], words[:, v * P : (v + 1) * P], identity)
+
+
+def planes_side_by_side(bank):
+    return bank.rearrange("p (g u) r -> p g r u", g=PASSES)
+
+
+def interleave_views(z_flat, y_chunk, first_channel, lo, hi):
+    dst = z_flat[:, TOKENS * (first_channel + lo) : TOKENS * (first_channel + hi)]
+    dst = dst.rearrange("p (c i n) -> p c n i", i=RUN, n=TOKENS)
+    src = y_chunk[:, :, lo:hi].rearrange("p n (c i) -> p c n i", i=RUN)
+    return dst, src
+
+
+def tile_attention_pa_kernel(tc, y_attn, w_proj, b_proj, out):
+    nc = tc.nc
+    out_rows = out.rearrange("b (a i) f -> (b a) i f", a=HALVES)
+    w_tiles = w_proj.rearrange("(t p) j -> p t j", p=P)
+
+    with tc.tile_pool(name="keep", bufs=1) as keep, tc.tile_pool(name="zq", bufs=LEAD + 2) as zq, tc.tile_pool(
+        name="results", bufs=4
+    ) as results, tc.psum_pool(name="planes", bufs=4) as planes, tc.psum_pool(name="sums", bufs=4) as sums:
+        w_raw = keep.tile([P, W_TILES, K], BF16)
+        bias_rows = keep.tile([P, FEATURES], BF16)
+        nc.vector.memset(bias_rows[:], 0.0)
+        half_w = W_TILES // N_TILES
+        nc.sync.dma_start(out=w_raw[:, 0:half_w, :], in_=w_tiles[:, 0:half_w, :])
+        nc.sync.dma_start(out=bias_rows[0:1, :], in_=b_proj.rearrange("(o f) -> o f", o=1))
+        y_chunks = []
+        first_channel = 0
+        for c, width in enumerate(CHUNKS):
+            y_chunk = keep.tile([P, TOKENS, width], BF16, name="y_chunk%d" % c)
+            for a in range(HALVES):
+                lo = a * HALF_CHANNELS + first_channel
+                nc.sync.dma_start(out=y_chunk[a:P:HALVES, :, :], in_=y_attn[:, :, lo : lo + width])
+            y_chunks.append((y_chunk, first_channel, width))
+            first_channel += width
+            if c == 0:
+                nc.sync.dma_start(out=w_raw[:, half_w:W_TILES, :], in_=w_tiles[:, half_w:W_TILES, :])
+
+        identity = keep.tile([P, P], F32)
+        make_identity(nc, identity[:])
+        ones = keep.tile([P, P], BF16)
+        nc.vector.memset(ones[:], 1.0)
+
+        bias = keep.tile([P, FEATURES], F32)
+        for h in range(N_TILES):
+            cols = slice(h * N_TILE, (h + 1) * N_TILE)
+            spread = sums.tile([P, N_TILE], F32, tag="acc")
+            nc.tensor.matmul(out=spread[:], lhsT=ones[:], rhs=bias_rows[:, cols], start=True, stop=True)
+            nc.vector.tensor_copy(out=bias[:, cols], in_=spread[:])
+
+        w_grouped = keep.tile([P, PASSES, FEATURES * PACK], BF16, align_bytes=64)
+        w_codes = keep.tile([P, PASSES, FEATURES], U32, align_bytes=64)
+        w_scales = keep.tile([P, PASSES, FEATURES], U8, align_bytes=64)
+        for t in range(W_TILES):
+            bank = planes.tile([P, PLANES, P], F32, tag="bank")
+            transpose_row_tile(nc, bank, w_raw[:, t, :], identity[:])
+            target = w_grouped[:, :, t * P * PACK : (t + 1) * P * PACK].bitcast(F32)
+            target = target.rearrange("p g (r u) -> p g r u", u=2)
+            if t % 2 == 0:
+                nc.vector.tensor_copy(out=target, in_=planes_side_by_side(bank))
+            else:
+                nc.scalar.copy(out=target, in_=planes_side_by_side(bank))
+            if (t + 1) % half_w == 0:
+                h = t // half_w
+                for g in range(PASSES):
+                    nc.vector.quantize_mx(
+                        out=w_codes[:, g, h * N_TILE : (h + 1) * N_TILE].bitcast(FP8X4),
+                        scales=w_scales[:, g, h * N_TILE : (h + 1) * N_TILE],
+                        in_=w_grouped[:, g, h * N_TILE * PACK : (h + 1) * N_TILE * PACK],
+                    )
+
+        z_flat = keep.tile([P, ROWS * K], BF16, align_bytes=64)
+        for c, (y_chunk, first_channel, width) in enumerate(y_chunks):
+            for lo in range(0, width, UNIT):
+                if c == 0:
+                    dst, src = interleave_views(z_flat, y_chunk, first_channel, lo, lo + UNIT)
+                    nc.vector.tensor_copy(out=dst, in_=src)
+                else:
+                    mid = lo + UNIT // 2
+                    dst, src = interleave_views(z_flat, y_chunk, first_channel, lo, mid)
+                    nc.gpsimd.tensor_scalar(out=dst, in0=src, scalar1=1.0, scalar2=0.0, op0=MULT, op1=ADD)
+                    dst, src = interleave_views(z_flat, y_chunk, first_channel, mid, lo + UNIT)
+                    nc.scalar.copy(out=dst, in_=src)
+
+        groups = [(first, min(GROUP, ROWS - first)) for first in range(0, ROWS, GROUP)]
+        quantised = []
+
+        def prepare(first, count):
+            z_grouped = zq.tile([P, GROUP, PASSES, P * PACK], BF16, align_bytes=64)
+            for r in range(count):
+                bank = planes.tile([P, PLANES, P], F32, tag="bank")
+                transpose_row_tile(nc, bank, z_flat[:, (first + r) * K : (first + r + 1) * K], identity[:])
+                target = z_grouped[:, r, :, :].bitcast(F32).rearrange("p g (r u) -> p g r u", u=2)
+                nc.scalar.copy(out=target, in_=planes_side_by_side(bank))
+            z_codes = zq.tile([P, GROUP * PASSES * P], U32, align_bytes=64)
+            z_scales = zq.tile([P, GROUP * PASSES * P], U8, align_bytes=64)
+            used = count * PASSES * P
+            nc.vector.quantize_mx(
+                out=z_codes[:, 0:used].bitcast(FP8X4),
+                scales=z_scales[:, 0:used],
+                in_=z_grouped[:, 0:count, :, :].rearrange("p r g x -> p (r g x)"),
+            )
+            quantised.append((z_codes, z_scales))
+
+        def multiply(index, first, count):
+            z_codes, z_scales = quantised[index]
+            result = results.tile([P, GROUP, FEATURES], F32)
+            for r in range(count):
+                for h in range(N_TILES):
+                    cols = slice(h * N_TILE, (h + 1) * N_TILE)
+                    acc = sums.tile([P, N_TILE], F32, tag="acc")
+                    for g in range(PASSES):
+                        z_cols = slice((r * PASSES + g) * P, (r * PASSES + g + 1) * P)
+                        nc.tensor.matmul_mx(
+                            out=acc[:],
+                            lhsT=z_codes[:, z_cols].bitcast(FP8X4),
+                            lhsT_scale=z_scales[:, z_cols],
+                            rhs=w_codes[:, g, cols].bitcast(FP8X4),
+                            rhs_scale=w_scales[:, g, cols],
+                            start=(g == 0),
+                            stop=(g == PASSES - 1),
+                        )
+                    nc.vector.tensor_tensor(out=result[:, r, cols], in0=acc[:], in1=bias[:, cols], op=ADD)
+            nc.sync.dma_start(out=out_rows[:, first : first + count, :], in_=result[:, 0:count, :])
+
+        for step in range(len(groups) + LEAD):
+            if step < len(groups):
+                prepare(groups[step][0], groups[step][1])
+            if step >= LEAD:
+                multiply(step - LEAD, groups[step - LEAD][0], groups[step - LEAD][1])

@@ -26,11 +26,13 @@ PLANES = WORDS // P
 N_TILE = 512
 N_TILES = FEATURES // N_TILE
 W_TILES = FEATURES // P
-CHUNKS = (128, 128, 256)
+CHUNK = 256
 UNIT = 32
+UNITS = HALF_CHANNELS // UNIT
 RUN = 4
 GROUP = 2
 LEAD = 2
+AHEAD = 1
 
 FLOPS = 2 * IMAGES * TOKENS * K * FEATURES
 
@@ -52,43 +54,41 @@ def interleave_views(z_flat, y_chunk, first_channel, lo, hi):
     return dst, src
 
 
+def units_for_rows(rows):
+    return min(UNITS, -(-rows * K // (TOKENS * UNIT)))
+
+
 def tile_attention_pa_kernel(tc, y_attn, w_proj, b_proj, out):
     nc = tc.nc
     out_rows = out.rearrange("b (a i) f -> (b a) i f", a=HALVES)
     w_tiles = w_proj.rearrange("(t p) j -> p t j", p=P)
+    half_w = W_TILES // N_TILES
 
     with tc.tile_pool(name="keep", bufs=1) as keep, tc.tile_pool(name="zq", bufs=LEAD + 2) as zq, tc.tile_pool(
-        name="results", bufs=4
-    ) as results, tc.psum_pool(name="planes", bufs=4) as planes, tc.psum_pool(name="sums", bufs=4) as sums:
-        w_raw = keep.tile([P, W_TILES, K], BF16)
+        name="results", bufs=5
+    ) as results, tc.psum_pool(name="planes", bufs=4) as planes, tc.psum_pool(
+        name="sums", bufs=4
+    ) as sums, tc.manual_schedule():
         bias_rows = keep.tile([P, FEATURES], BF16)
         nc.vector.memset(bias_rows[:], 0.0)
-        half_w = W_TILES // N_TILES
-        nc.sync.dma_start(out=w_raw[:, 0:half_w, :], in_=w_tiles[:, 0:half_w, :])
-        nc.sync.dma_start(out=bias_rows[0:1, :], in_=b_proj.rearrange("(o f) -> o f", o=1))
-        y_chunks = []
-        first_channel = 0
-        for c, width in enumerate(CHUNKS):
-            y_chunk = keep.tile([P, TOKENS, width], BF16, name="y_chunk%d" % c)
-            for a in range(HALVES):
-                lo = a * HALF_CHANNELS + first_channel
-                nc.sync.dma_start(out=y_chunk[a:P:HALVES, :, :], in_=y_attn[:, :, lo : lo + width])
-            y_chunks.append((y_chunk, first_channel, width))
-            first_channel += width
-            if c == 0:
-                nc.sync.dma_start(out=w_raw[:, half_w:W_TILES, :], in_=w_tiles[:, half_w:W_TILES, :])
-
-        identity = keep.tile([P, P], F32)
-        make_identity(nc, identity[:])
         ones = keep.tile([P, P], BF16)
         nc.vector.memset(ones[:], 1.0)
+        identity = keep.tile([P, P], F32)
+        make_identity(nc, identity[:])
 
-        bias = keep.tile([P, FEATURES], F32)
+        w_raw = keep.tile([P, W_TILES, K], BF16)
         for h in range(N_TILES):
-            cols = slice(h * N_TILE, (h + 1) * N_TILE)
-            spread = sums.tile([P, N_TILE], F32, tag="acc")
-            nc.tensor.matmul(out=spread[:], lhsT=ones[:], rhs=bias_rows[:, cols], start=True, stop=True)
-            nc.vector.tensor_copy(out=bias[:, cols], in_=spread[:])
+            nc.sync.dma_start(
+                out=w_raw[:, h * half_w : (h + 1) * half_w, :], in_=w_tiles[:, h * half_w : (h + 1) * half_w, :]
+            )
+        nc.sync.dma_start(out=bias_rows[0:1, :], in_=b_proj.rearrange("(o f) -> o f", o=1))
+        y_chunks = []
+        for c in range(HALF_CHANNELS // CHUNK):
+            y_chunk = keep.tile([P, TOKENS, CHUNK], BF16, name="y_chunk%d" % c)
+            for a in range(HALVES):
+                lo = a * HALF_CHANNELS + c * CHUNK
+                nc.sync.dma_start(out=y_chunk[a:P:HALVES, :, :], in_=y_attn[:, :, lo : lo + CHUNK])
+            y_chunks.append(y_chunk)
 
         w_grouped = keep.tile([P, PASSES, FEATURES * PACK], BF16, align_bytes=64)
         w_codes = keep.tile([P, PASSES, FEATURES], U32, align_bytes=64)
@@ -111,21 +111,30 @@ def tile_attention_pa_kernel(tc, y_attn, w_proj, b_proj, out):
                         in_=w_grouped[:, g, h * N_TILE * PACK : (h + 1) * N_TILE * PACK],
                     )
 
-        z_flat = keep.tile([P, ROWS * K], BF16, align_bytes=64)
-        for c, (y_chunk, first_channel, width) in enumerate(y_chunks):
-            for lo in range(0, width, UNIT):
-                if c == 0:
-                    dst, src = interleave_views(z_flat, y_chunk, first_channel, lo, lo + UNIT)
-                    nc.vector.tensor_copy(out=dst, in_=src)
-                else:
-                    mid = lo + UNIT // 2
-                    dst, src = interleave_views(z_flat, y_chunk, first_channel, lo, mid)
-                    nc.gpsimd.tensor_scalar(out=dst, in0=src, scalar1=1.0, scalar2=0.0, op0=MULT, op1=ADD)
-                    dst, src = interleave_views(z_flat, y_chunk, first_channel, mid, lo + UNIT)
-                    nc.scalar.copy(out=dst, in_=src)
+        bias = keep.tile([P, FEATURES], F32)
+        for h in range(N_TILES):
+            cols = slice(h * N_TILE, (h + 1) * N_TILE)
+            spread = sums.tile([P, N_TILE], F32, tag="acc")
+            nc.tensor.matmul(out=spread[:], lhsT=ones[:], rhs=bias_rows[:, cols], start=True, stop=True)
+            nc.vector.tensor_copy(out=bias[:, cols], in_=spread[:])
 
+        z_flat = keep.tile([P, ROWS * K], BF16, align_bytes=64)
         groups = [(first, min(GROUP, ROWS - first)) for first in range(0, ROWS, GROUP)]
         quantised = []
+
+        def interleave(unit, before_the_sums):
+            y_chunk = y_chunks[unit * UNIT // CHUNK]
+            first_channel = unit * UNIT // CHUNK * CHUNK
+            lo = unit * UNIT - first_channel
+            if before_the_sums:
+                dst, src = interleave_views(z_flat, y_chunk, first_channel, lo, lo + UNIT)
+                nc.vector.tensor_copy(out=dst, in_=src)
+            else:
+                mid = lo + UNIT // 2
+                dst, src = interleave_views(z_flat, y_chunk, first_channel, lo, mid)
+                nc.gpsimd.tensor_scalar(out=dst, in0=src, scalar1=1.0, scalar2=0.0, op0=MULT, op1=ADD)
+                dst, src = interleave_views(z_flat, y_chunk, first_channel, mid, lo + UNIT)
+                nc.scalar.copy(out=dst, in_=src)
 
         def prepare(first, count):
             z_grouped = zq.tile([P, GROUP, PASSES, P * PACK], BF16, align_bytes=64)
@@ -165,8 +174,14 @@ def tile_attention_pa_kernel(tc, y_attn, w_proj, b_proj, out):
                     nc.vector.tensor_tensor(out=result[:, r, cols], in0=acc[:], in1=bias[:, cols], op=ADD)
             nc.sync.dma_start(out=out_rows[:, first : first + count, :], in_=result[:, 0:count, :])
 
-        for step in range(len(groups) + LEAD):
-            if step < len(groups):
-                prepare(groups[step][0], groups[step][1])
-            if step >= LEAD:
-                multiply(step - LEAD, groups[step - LEAD][0], groups[step - LEAD][1])
+        def units_through(index):
+            return units_for_rows(groups[index][0] + groups[index][1]) if index >= 0 else 0
+
+        for step in range(-(LEAD + AHEAD), len(groups)):
+            if step + LEAD + AHEAD < len(groups):
+                for unit in range(units_through(step + LEAD + AHEAD - 1), units_through(step + LEAD + AHEAD)):
+                    interleave(unit, step < 0)
+            if 0 <= step + LEAD < len(groups):
+                prepare(groups[step + LEAD][0], groups[step + LEAD][1])
+            if step >= 0:
+                multiply(step, groups[step][0], groups[step][1])

@@ -26,13 +26,16 @@ PLANES = WORDS // P
 N_TILE = 512
 N_TILES = FEATURES // N_TILE
 W_TILES = FEATURES // P
-CHUNK = 256
-UNIT = 32
-UNITS = HALF_CHANNELS // UNIT
-RUN = 4
 GROUP = 2
-LEAD = 2
-AHEAD = 1
+LEAD = 1
+AHEAD = 2
+RUN = 4
+SLAB = 8
+CHUNKS = (128, 160, 224)
+VECTOR_FIRST = 24
+SCALAR_SHARE = 16
+GPSIMD_SHARE = 8
+RESULT_ROWS = 14
 
 FLOPS = 2 * IMAGES * TOKENS * K * FEATURES
 
@@ -47,15 +50,8 @@ def planes_side_by_side(bank):
     return bank.rearrange("p (g u) r -> p g r u", g=PASSES)
 
 
-def interleave_views(z_flat, y_chunk, first_channel, lo, hi):
-    dst = z_flat[:, TOKENS * (first_channel + lo) : TOKENS * (first_channel + hi)]
-    dst = dst.rearrange("p (c i n) -> p c n i", i=RUN, n=TOKENS)
-    src = y_chunk[:, :, lo:hi].rearrange("p n (c i) -> p c n i", i=RUN)
-    return dst, src
-
-
-def units_for_rows(rows):
-    return min(UNITS, -(-rows * K // (TOKENS * UNIT)))
+def channels_through(rows):
+    return min(HALF_CHANNELS, -(-rows * K // (TOKENS * SLAB)) * SLAB)
 
 
 def tile_attention_pa_kernel(tc, y_attn, w_proj, b_proj, out):
@@ -65,7 +61,7 @@ def tile_attention_pa_kernel(tc, y_attn, w_proj, b_proj, out):
     half_w = W_TILES // N_TILES
 
     with tc.tile_pool(name="keep", bufs=1) as keep, tc.tile_pool(name="zq", bufs=LEAD + 2) as zq, tc.tile_pool(
-        name="results", bufs=5
+        name="results", bufs=RESULT_ROWS
     ) as results, tc.psum_pool(name="planes", bufs=4) as planes, tc.psum_pool(
         name="sums", bufs=4
     ) as sums, tc.manual_schedule():
@@ -83,12 +79,14 @@ def tile_attention_pa_kernel(tc, y_attn, w_proj, b_proj, out):
             )
         nc.sync.dma_start(out=bias_rows[0:1, :], in_=b_proj.rearrange("(o f) -> o f", o=1))
         y_chunks = []
-        for c in range(HALF_CHANNELS // CHUNK):
-            y_chunk = keep.tile([P, TOKENS, CHUNK], BF16, name="y_chunk%d" % c)
+        first_channel = 0
+        for c, width in enumerate(CHUNKS):
+            y_chunk = keep.tile([P, TOKENS, width], BF16, name="y_chunk%d" % c)
             for a in range(HALVES):
-                lo = a * HALF_CHANNELS + c * CHUNK
-                nc.sync.dma_start(out=y_chunk[a:P:HALVES, :, :], in_=y_attn[:, :, lo : lo + CHUNK])
-            y_chunks.append(y_chunk)
+                lo = a * HALF_CHANNELS + first_channel
+                nc.sync.dma_start(out=y_chunk[a:P:HALVES, :, :], in_=y_attn[:, :, lo : lo + width])
+            y_chunks.append((y_chunk, first_channel, width))
+            first_channel += width
 
         w_grouped = keep.tile([P, PASSES, FEATURES * PACK], BF16, align_bytes=64)
         w_codes = keep.tile([P, PASSES, FEATURES], U32, align_bytes=64)
@@ -120,68 +118,82 @@ def tile_attention_pa_kernel(tc, y_attn, w_proj, b_proj, out):
 
         z_flat = keep.tile([P, ROWS * K], BF16, align_bytes=64)
         groups = [(first, min(GROUP, ROWS - first)) for first in range(0, ROWS, GROUP)]
-        quantised = []
+        quantised = {}
 
-        def interleave(unit, before_the_sums):
-            y_chunk = y_chunks[unit * UNIT // CHUNK]
-            first_channel = unit * UNIT // CHUNK * CHUNK
-            lo = unit * UNIT - first_channel
+        def interleave_views(lo, hi):
+            y_chunk, first_channel, width = [c for c in y_chunks if c[1] <= lo < c[1] + c[2]][0]
+            assert hi <= first_channel + width
+            dst = z_flat[:, TOKENS * lo : TOKENS * hi].rearrange("p (c i n) -> p c n i", i=RUN, n=TOKENS)
+            src = y_chunk[:, :, lo - first_channel : hi - first_channel].rearrange("p n (c i) -> p c n i", i=RUN)
+            return dst, src
+
+        def interleave(index, before_the_sums):
+            lo = channels_through(groups[index][0])
+            hi = channels_through(groups[index][0] + groups[index][1])
             if before_the_sums:
-                dst, src = interleave_views(z_flat, y_chunk, first_channel, lo, lo + UNIT)
+                vector_end = min(hi, lo + VECTOR_FIRST)
+                dst, src = interleave_views(lo, vector_end)
                 nc.vector.tensor_copy(out=dst, in_=src)
+                if vector_end < hi:
+                    dst, src = interleave_views(vector_end, hi)
+                    nc.scalar.copy(out=dst, in_=src)
             else:
-                mid = lo + UNIT // 2
-                dst, src = interleave_views(z_flat, y_chunk, first_channel, lo, mid)
-                nc.gpsimd.tensor_scalar(out=dst, in0=src, scalar1=1.0, scalar2=0.0, op0=MULT, op1=ADD)
-                dst, src = interleave_views(z_flat, y_chunk, first_channel, mid, lo + UNIT)
+                scalar_end = min(hi, lo + SCALAR_SHARE)
+                dst, src = interleave_views(lo, scalar_end)
                 nc.scalar.copy(out=dst, in_=src)
+                gpsimd_end = min(hi, scalar_end + GPSIMD_SHARE)
+                if scalar_end < gpsimd_end:
+                    dst, src = interleave_views(scalar_end, gpsimd_end)
+                    nc.gpsimd.tensor_scalar(out=dst, in0=src, scalar1=1.0, scalar2=0.0, op0=MULT, op1=ADD)
+                if gpsimd_end < hi:
+                    dst, src = interleave_views(gpsimd_end, hi)
+                    nc.vector.tensor_copy(out=dst, in_=src)
 
-        def prepare(first, count):
-            z_grouped = zq.tile([P, GROUP, PASSES, P * PACK], BF16, align_bytes=64)
+        def prepare(index):
+            first, count = groups[index]
+            z_grouped = zq.tile([P, GROUP, PASSES * P * PACK], BF16, align_bytes=64)
+            z_codes = zq.tile([P, GROUP, PASSES * P], U32, align_bytes=64)
+            z_scales = zq.tile([P, GROUP, PASSES * P], U8, align_bytes=64)
             for r in range(count):
                 bank = planes.tile([P, PLANES, P], F32, tag="bank")
                 transpose_row_tile(nc, bank, z_flat[:, (first + r) * K : (first + r + 1) * K], identity[:])
-                target = z_grouped[:, r, :, :].bitcast(F32).rearrange("p g (r u) -> p g r u", u=2)
+                target = z_grouped[:, r, :].bitcast(F32).rearrange("p (g r u) -> p g r u", g=PASSES, u=2)
                 nc.scalar.copy(out=target, in_=planes_side_by_side(bank))
-            z_codes = zq.tile([P, GROUP * PASSES * P], U32, align_bytes=64)
-            z_scales = zq.tile([P, GROUP * PASSES * P], U8, align_bytes=64)
-            used = count * PASSES * P
-            nc.vector.quantize_mx(
-                out=z_codes[:, 0:used].bitcast(FP8X4),
-                scales=z_scales[:, 0:used],
-                in_=z_grouped[:, 0:count, :, :].rearrange("p r g x -> p (r g x)"),
-            )
-            quantised.append((z_codes, z_scales))
-
-        def multiply(index, first, count):
-            z_codes, z_scales = quantised[index]
-            result = results.tile([P, GROUP, FEATURES], F32)
             for r in range(count):
+                nc.vector.quantize_mx(
+                    out=z_codes[:, r, :].bitcast(FP8X4), scales=z_scales[:, r, :], in_=z_grouped[:, r, :]
+                )
+            quantised[index] = (z_codes, z_scales)
+
+        def multiply(index):
+            first, count = groups[index]
+            z_codes, z_scales = quantised[index]
+            for r in range(count):
+                result = results.tile([P, FEATURES], F32)
                 for h in range(N_TILES):
                     cols = slice(h * N_TILE, (h + 1) * N_TILE)
                     acc = sums.tile([P, N_TILE], F32, tag="acc")
                     for g in range(PASSES):
-                        z_cols = slice((r * PASSES + g) * P, (r * PASSES + g + 1) * P)
                         nc.tensor.matmul_mx(
                             out=acc[:],
-                            lhsT=z_codes[:, z_cols].bitcast(FP8X4),
-                            lhsT_scale=z_scales[:, z_cols],
+                            lhsT=z_codes[:, r, g * P : (g + 1) * P].bitcast(FP8X4),
+                            lhsT_scale=z_scales[:, r, g * P : (g + 1) * P],
                             rhs=w_codes[:, g, cols].bitcast(FP8X4),
                             rhs_scale=w_scales[:, g, cols],
                             start=(g == 0),
                             stop=(g == PASSES - 1),
                         )
-                    nc.vector.tensor_tensor(out=result[:, r, cols], in0=acc[:], in1=bias[:, cols], op=ADD)
-            nc.sync.dma_start(out=out_rows[:, first : first + count, :], in_=result[:, 0:count, :])
-
-        def units_through(index):
-            return units_for_rows(groups[index][0] + groups[index][1]) if index >= 0 else 0
+                    if r == 1 and h == 0:
+                        nc.scalar.copy(out=result[:, cols], in_=acc[:])
+                        nc.gpsimd.tensor_tensor(out=result[:, cols], in0=result[:, cols], in1=bias[:, cols], op=ADD)
+                    else:
+                        nc.vector.tensor_tensor(out=result[:, cols], in0=acc[:], in1=bias[:, cols], op=ADD)
+                nc.sync.dma_start(out=out_rows[:, first + r, :], in_=result[:])
 
         for step in range(-(LEAD + AHEAD), len(groups)):
-            if step + LEAD + AHEAD < len(groups):
-                for unit in range(units_through(step + LEAD + AHEAD - 1), units_through(step + LEAD + AHEAD)):
-                    interleave(unit, step < 0)
             if 0 <= step + LEAD < len(groups):
-                prepare(groups[step + LEAD][0], groups[step + LEAD][1])
+                prepare(step + LEAD)
             if step >= 0:
-                multiply(step, groups[step][0], groups[step][1])
+                multiply(step)
+            if step + LEAD + AHEAD < len(groups):
+                interleave(step + LEAD + AHEAD, step < 0)

@@ -30,10 +30,9 @@ GROUP = 2
 LEAD = 1
 AHEAD = 2
 RUN = 4
-SLAB = 8
-CHUNKS = (128, 160, 224)
-VECTOR_FIRST = 24
-SCALAR_SHARE = 16
+SLAB = 16
+CHUNKS = (128, 128, 256)
+VECTOR_FIRST = 32
 GPSIMD_SHARE = 8
 RESULT_ROWS = 14
 
@@ -138,7 +137,7 @@ def tile_attention_pa_kernel(tc, y_attn, w_proj, b_proj, out):
                     dst, src = interleave_views(vector_end, hi)
                     nc.scalar.copy(out=dst, in_=src)
             else:
-                scalar_end = min(hi, lo + SCALAR_SHARE)
+                scalar_end = lo + (hi - lo) // 2
                 dst, src = interleave_views(lo, scalar_end)
                 nc.scalar.copy(out=dst, in_=src)
                 gpsimd_end = min(hi, scalar_end + GPSIMD_SHARE)

@@ -7,7 +7,6 @@ U32 = mybir.dt.uint32
 U8 = mybir.dt.uint8
 FP8X4 = mybir.dt.float8_e4m3fn_x4
 ADD = mybir.AluOpType.add
-MULT = mybir.AluOpType.mult
 
 P = 128
 IMAGES = 64
@@ -27,13 +26,10 @@ N_TILE = 512
 N_TILES = FEATURES // N_TILE
 W_TILES = FEATURES // P
 GROUP = 2
-LEAD = 1
-AHEAD = 2
 RUN = 4
 SLAB = 16
 CHUNKS = (128, 128, 256)
 VECTOR_FIRST = 32
-GPSIMD_SHARE = 8
 RESULT_ROWS = 14
 
 FLOPS = 2 * IMAGES * TOKENS * K * FEATURES
@@ -56,10 +52,8 @@ def channels_through(rows):
 def tile_attention_pa_kernel(tc, y_attn, w_proj, b_proj, out):
     nc = tc.nc
     out_rows = out.rearrange("b (a i) f -> (b a) i f", a=HALVES)
-    w_tiles = w_proj.rearrange("(t p) j -> p t j", p=P)
-    half_w = W_TILES // N_TILES
 
-    with tc.tile_pool(name="keep", bufs=1) as keep, tc.tile_pool(name="zq", bufs=LEAD + 2) as zq, tc.tile_pool(
+    with tc.tile_pool(name="keep", bufs=1) as keep, tc.tile_pool(name="zq", bufs=3) as zq, tc.tile_pool(
         name="results", bufs=RESULT_ROWS
     ) as results, tc.psum_pool(name="planes", bufs=4) as planes, tc.psum_pool(
         name="sums", bufs=4
@@ -72,10 +66,7 @@ def tile_attention_pa_kernel(tc, y_attn, w_proj, b_proj, out):
         make_identity(nc, identity[:])
 
         w_raw = keep.tile([P, W_TILES, K], BF16)
-        for h in range(N_TILES):
-            nc.sync.dma_start(
-                out=w_raw[:, h * half_w : (h + 1) * half_w, :], in_=w_tiles[:, h * half_w : (h + 1) * half_w, :]
-            )
+        nc.sync.dma_start(out=w_raw[:], in_=w_proj.rearrange("(r t) j -> r t j", t=W_TILES))
         nc.sync.dma_start(out=bias_rows[0:1, :], in_=b_proj.rearrange("(o f) -> o f", o=1))
         y_chunks = []
         first_channel = 0
@@ -90,23 +81,23 @@ def tile_attention_pa_kernel(tc, y_attn, w_proj, b_proj, out):
         w_grouped = keep.tile([P, PASSES, FEATURES * PACK], BF16, align_bytes=64)
         w_codes = keep.tile([P, PASSES, FEATURES], U32, align_bytes=64)
         w_scales = keep.tile([P, PASSES, FEATURES], U8, align_bytes=64)
-        for t in range(W_TILES):
-            bank = planes.tile([P, PLANES, P], F32, tag="bank")
-            transpose_row_tile(nc, bank, w_raw[:, t, :], identity[:])
-            target = w_grouped[:, :, t * P * PACK : (t + 1) * P * PACK].bitcast(F32)
-            target = target.rearrange("p g (r u) -> p g r u", u=2)
-            if t % 2 == 0:
-                nc.vector.tensor_copy(out=target, in_=planes_side_by_side(bank))
-            else:
-                nc.scalar.copy(out=target, in_=planes_side_by_side(bank))
-            if (t + 1) % half_w == 0:
-                h = t // half_w
-                for g in range(PASSES):
-                    nc.vector.quantize_mx(
-                        out=w_codes[:, g, h * N_TILE : (h + 1) * N_TILE].bitcast(FP8X4),
-                        scales=w_scales[:, g, h * N_TILE : (h + 1) * N_TILE],
-                        in_=w_grouped[:, g, h * N_TILE * PACK : (h + 1) * N_TILE * PACK],
-                    )
+        for g in range(PASSES):
+            for t in range(0, W_TILES, 2):
+                bank = planes.tile([P, PLANES, P], F32, tag="bank")
+                for i in range(2):
+                    words = w_raw[:, t + i, :].bitcast(F32)
+                    for u in range(2):
+                        v = 2 * g + u
+                        nc.tensor.transpose(bank[:, 2 * i + u, :], words[:, v * P : (v + 1) * P], identity[:])
+                target = w_grouped[:, g, :].bitcast(F32).rearrange("p (r t u) -> p r t u", t=W_TILES, u=2)
+                source = bank.rearrange("p (i u) r -> p r i u", u=2)
+                if t < W_TILES // 2:
+                    nc.vector.tensor_copy(out=target[:, :, t : t + 2, :], in_=source)
+                else:
+                    nc.scalar.copy(out=target[:, :, t : t + 2, :], in_=source)
+            nc.vector.quantize_mx(
+                out=w_codes[:, g, :].bitcast(FP8X4), scales=w_scales[:, g, :], in_=w_grouped[:, g, :]
+            )
 
         bias = keep.tile([P, FEATURES], F32)
         for h in range(N_TILES):
@@ -140,13 +131,8 @@ def tile_attention_pa_kernel(tc, y_attn, w_proj, b_proj, out):
                 scalar_end = lo + (hi - lo) // 2
                 dst, src = interleave_views(lo, scalar_end)
                 nc.scalar.copy(out=dst, in_=src)
-                gpsimd_end = min(hi, scalar_end + GPSIMD_SHARE)
-                if scalar_end < gpsimd_end:
-                    dst, src = interleave_views(scalar_end, gpsimd_end)
-                    nc.gpsimd.tensor_scalar(out=dst, in0=src, scalar1=1.0, scalar2=0.0, op0=MULT, op1=ADD)
-                if gpsimd_end < hi:
-                    dst, src = interleave_views(gpsimd_end, hi)
-                    nc.vector.tensor_copy(out=dst, in_=src)
+                dst, src = interleave_views(scalar_end, hi)
+                nc.vector.tensor_copy(out=dst, in_=src)
 
         def prepare(index):
             first, count = groups[index]
@@ -189,10 +175,13 @@ def tile_attention_pa_kernel(tc, y_attn, w_proj, b_proj, out):
                         nc.vector.tensor_tensor(out=result[:, cols], in0=acc[:], in1=bias[:, cols], op=ADD)
                 nc.sync.dma_start(out=out_rows[:, first + r, :], in_=result[:])
 
-        for step in range(-(LEAD + AHEAD), len(groups)):
-            if 0 <= step + LEAD < len(groups):
-                prepare(step + LEAD)
-            if step >= 0:
-                multiply(step)
-            if step + LEAD + AHEAD < len(groups):
-                interleave(step + LEAD + AHEAD, step < 0)
+        first_batches = len([g for g in groups if channels_through(g[0] + g[1]) <= CHUNKS[0]])
+        for index in range(first_batches):
+            interleave(index, True)
+        prepare(0)
+        for step in range(len(groups)):
+            if step + 1 < len(groups):
+                prepare(step + 1)
+            if first_batches <= step + 2 < len(groups):
+                interleave(step + 2, False)
+            multiply(step)

import concourse.mybir as mybir
from concourse.masks import make_identity

F32 = mybir.dt.float32
BF16 = mybir.dt.bfloat16
U32 = mybir.dt.uint32
U8 = mybir.dt.uint8
FP8X4 = mybir.dt.float8_e4m3fn_x4
ADD = mybir.AluOpType.add

P = 128
IMAGES = 64
TOKENS = 50
CHANNELS = 1024
FEATURES = 1024
K = 1024
HALVES = 2
HALF_CHANNELS = CHANNELS // HALVES
ROWS = TOKENS // HALVES
PACK = 4
K_PASS = P * PACK
PASSES = K // K_PASS
WORDS = K // 2
PLANES = WORDS // P
N_TILE = 512
N_TILES = FEATURES // N_TILE
W_TILES = FEATURES // P
GROUP = 2
RUN = 4
SLAB = 16
CHUNKS = (128, 128, 256)
VECTOR_FIRST = 32
RESULT_ROWS = 14

FLOPS = 2 * IMAGES * TOKENS * K * FEATURES


def transpose_row_tile(nc, bank, rows_bf16, identity):
    words = rows_bf16.bitcast(F32)
    for v in range(PLANES):
        nc.tensor.transpose(bank[:, v, :], words[:, v * P : (v + 1) * P], identity)


def planes_side_by_side(bank):
    return bank.rearrange("p (g u) r -> p g r u", g=PASSES)


def channels_through(rows):
    return min(HALF_CHANNELS, -(-rows * K // (TOKENS * SLAB)) * SLAB)


def tile_attention_pa_kernel(tc, y_attn, w_proj, b_proj, out):
    nc = tc.nc
    out_rows = out.rearrange("b (a i) f -> (b a) i f", a=HALVES)

    with tc.tile_pool(name="keep", bufs=1) as keep, tc.tile_pool(name="zq", bufs=3) as zq, tc.tile_pool(
        name="results", bufs=RESULT_ROWS
    ) as results, tc.psum_pool(name="planes", bufs=4) as planes, tc.psum_pool(
        name="sums", bufs=4
    ) as sums, tc.manual_schedule():
        bias_rows = keep.tile([P, FEATURES], BF16)
        nc.vector.memset(bias_rows[:], 0.0)
        ones = keep.tile([P, P], BF16)
        nc.vector.memset(ones[:], 1.0)
        identity = keep.tile([P, P], F32)
        make_identity(nc, identity[:])

        w_raw = keep.tile([P, W_TILES, K], BF16)
        nc.sync.dma_start(out=w_raw[:], in_=w_proj.rearrange("(r t) j -> r t j", t=W_TILES))
        nc.sync.dma_start(out=bias_rows[0:1, :], in_=b_proj.rearrange("(o f) -> o f", o=1))
        y_chunks = []
        first_channel = 0
        for c, width in enumerate(CHUNKS):
            y_chunk = keep.tile([P, TOKENS, width], BF16, name="y_chunk%d" % c)
            for a in range(HALVES):
                lo = a * HALF_CHANNELS + first_channel
                nc.sync.dma_start(out=y_chunk[a:P:HALVES, :, :], in_=y_attn[:, :, lo : lo + width])
            y_chunks.append((y_chunk, first_channel, width))
            first_channel += width

        w_grouped = keep.tile([P, PASSES, FEATURES * PACK], BF16, align_bytes=64)
        w_codes = keep.tile([P, PASSES, FEATURES], U32, align_bytes=64)
        w_scales = keep.tile([P, PASSES, FEATURES], U8, align_bytes=64)
        for g in range(PASSES):
            for t in range(0, W_TILES, 2):
                bank = planes.tile([P, PLANES, P], F32, tag="bank")
                for i in range(2):
                    words = w_raw[:, t + i, :].bitcast(F32)
                    for u in range(2):
                        v = 2 * g + u
                        nc.tensor.transpose(bank[:, 2 * i + u, :], words[:, v * P : (v + 1) * P], identity[:])
                target = w_grouped[:, g, :].bitcast(F32).rearrange("p (r t u) -> p r t u", t=W_TILES, u=2)
                source = bank.rearrange("p (i u) r -> p r i u", u=2)
                if t < W_TILES // 2:
                    nc.vector.tensor_copy(out=target[:, :, t : t + 2, :], in_=source)
                else:
                    nc.scalar.copy(out=target[:, :, t : t + 2, :], in_=source)
            nc.vector.quantize_mx(
                out=w_codes[:, g, :].bitcast(FP8X4), scales=w_scales[:, g, :], in_=w_grouped[:, g, :]
            )

        bias = keep.tile([P, FEATURES], F32)
        for h in range(N_TILES):
            cols = slice(h * N_TILE, (h + 1) * N_TILE)
            spread = sums.tile([P, N_TILE], F32, tag="acc")
            nc.tensor.matmul(out=spread[:], lhsT=ones[:], rhs=bias_rows[:, cols], start=True, stop=True)
            nc.vector.tensor_copy(out=bias[:, cols], in_=spread[:])

        z_flat = keep.tile([P, ROWS * K], BF16, align_bytes=64)
        groups = [(first, min(GROUP, ROWS - first)) for first in range(0, ROWS, GROUP)]
        quantised = {}

        def interleave_views(lo, hi):
            y_chunk, first_channel, width = [c for c in y_chunks if c[1] <= lo < c[1] + c[2]][0]
            assert hi <= first_channel + width
            dst = z_flat[:, TOKENS * lo : TOKENS * hi].rearrange("p (c i n) -> p c n i", i=RUN, n=TOKENS)
            src = y_chunk[:, :, lo - first_channel : hi - first_channel].rearrange("p n (c i) -> p c n i", i=RUN)
            return dst, src

        def interleave(index, before_the_sums):
            lo = channels_through(groups[index][0])
            hi = channels_through(groups[index][0] + groups[index][1])
            if before_the_sums:
                vector_end = min(hi, lo + VECTOR_FIRST)
                dst, src = interleave_views(lo, vector_end)
                nc.vector.tensor_copy(out=dst, in_=src)
                if vector_end < hi:
                    dst, src = interleave_views(vector_end, hi)
                    nc.scalar.copy(out=dst, in_=src)
            else:
                scalar_end = lo + (hi - lo) // 2
                dst, src = interleave_views(lo, scalar_end)
                nc.scalar.copy(out=dst, in_=src)
                dst, src = interleave_views(scalar_end, hi)
                nc.vector.tensor_copy(out=dst, in_=src)

        def prepare(index):
            first, count = groups[index]
            z_grouped = zq.tile([P, GROUP, PASSES * P * PACK], BF16, align_bytes=64)
            z_codes = zq.tile([P, GROUP, PASSES * P], U32, align_bytes=64)
            z_scales = zq.tile([P, GROUP, PASSES * P], U8, align_bytes=64)
            for r in range(count):
                bank = planes.tile([P, PLANES, P], F32, tag="bank")
                transpose_row_tile(nc, bank, z_flat[:, (first + r) * K : (first + r + 1) * K], identity[:])
                target = z_grouped[:, r, :].bitcast(F32).rearrange("p (g r u) -> p g r u", g=PASSES, u=2)
                nc.scalar.copy(out=target, in_=planes_side_by_side(bank))
            for r in range(count):
                nc.vector.quantize_mx(
                    out=z_codes[:, r, :].bitcast(FP8X4), scales=z_scales[:, r, :], in_=z_grouped[:, r, :]
                )
            quantised[index] = (z_codes, z_scales)

        def multiply(index):
            first, count = groups[index]
            z_codes, z_scales = quantised[index]
            for r in range(count):
                result = results.tile([P, FEATURES], F32)
                for h in range(N_TILES):
                    cols = slice(h * N_TILE, (h + 1) * N_TILE)
                    acc = sums.tile([P, N_TILE], F32, tag="acc")
                    for g in range(PASSES):
                        nc.tensor.matmul_mx(
                            out=acc[:],
                            lhsT=z_codes[:, r, g * P : (g + 1) * P].bitcast(FP8X4),
                            lhsT_scale=z_scales[:, r, g * P : (g + 1) * P],
                            rhs=w_codes[:, g, cols].bitcast(FP8X4),
                            rhs_scale=w_scales[:, g, cols],
                            start=(g == 0),
                            stop=(g == PASSES - 1),
                        )
                    if r == 1 and h == 0:
                        nc.scalar.copy(out=result[:, cols], in_=acc[:])
                        nc.gpsimd.tensor_tensor(out=result[:, cols], in0=result[:, cols], in1=bias[:, cols], op=ADD)
                    else:
                        nc.vector.tensor_tensor(out=result[:, cols], in0=acc[:], in1=bias[:, cols], op=ADD)
                nc.sync.dma_start(out=out_rows[:, first + r, :], in_=result[:])

        first_batches = len([g for g in groups if channels_through(g[0] + g[1]) <= CHUNKS[0]])
        for index in range(first_batches):
            interleave(index, True)
        prepare(0)
        for step in range(len(groups)):
            if step + 1 < len(groups):
                prepare(step + 1)
            if first_batches <= step + 2 < len(groups):
                interleave(step + 2, False)
            multiply(step)
